import numpy as np
import ml_dtypes


def mxq(x, axis, fmt="e4m3"):
    dtype, down = {"e4m3": (ml_dtypes.float8_e4m3fn, 7), "e5m2": (ml_dtypes.float8_e5m2, 14)}[fmt]
    v = np.moveaxis(np.asarray(x, np.float32).astype(ml_dtypes.bfloat16).astype(np.float64), axis, -1)
    blocks = v.reshape(v.shape[:-1] + (-1, 32))
    amax = np.abs(blocks).max(-1, keepdims=True)
    byte = np.maximum(np.where(amax > 0, np.frexp(amax)[1] - 1 + 127, 0) - down, 1)
    scale = np.exp2(byte - 127.0)
    codes = (blocks / scale).astype(np.float32).astype(dtype).astype(np.float64)
    return np.moveaxis((codes * scale).reshape(v.shape), -1, axis)


WIDE = False


def mx_kscale(k):
    if not WIDE:
        return np.ones(k)
    levels = np.array([10, -10, 5, -5, 0])
    if k % 512:
        return np.exp2(np.random.permutation(np.resize(levels, k // 32))).repeat(32)
    a = np.empty((k // 512, 16))
    for p in range(k // 512):
        a[p, :8] = np.random.permutation(np.resize(levels, 8))
        for g in range(8):
            far = levels[np.abs(levels - a[p, g]) >= 10]
            a[p, g + 8] = far[np.random.randint(len(far))]
    return np.exp2(a.ravel()).repeat(32)


BF16 = ml_dtypes.bfloat16


def bf(x):
    return np.asarray(x, np.float32).astype(BF16)


def f64(x):
    return np.asarray(x).astype(np.float64)


N, D, L = 1024, 1024, 4
EPS = 1e-5
SLOPE = 0.1


def leaky(v):
    return np.where(v >= 0, v, SLOPE * v)


def layernorm(h, g, b):
    mu = np.mean(h, axis=-1, keepdims=True)
    var = np.mean((h - mu) ** 2, axis=-1, keepdims=True)
    return (h - mu) * (1.0 / np.sqrt(var + EPS)) * g + b


def setup_inputs():
    s, t = mx_kscale(N), mx_kscale(D)
    g = np.random.standard_normal((N, N))
    sq = (g * g.T) ** 2
    lap = 0.5 * (sq / sq.sum(axis=1, keepdims=True) + np.eye(N))
    feat = leaky(np.random.standard_normal((N, D)))
    return {"lap": bf(lap * s[None, :]),
            "feat": bf(feat / s[:, None] * t[None, :]),
            "w": bf(np.random.standard_normal((D, D)) / np.sqrt(D) / t[None, :]),
            "gamma": bf(1.0 + 0.1 * np.random.standard_normal(D)),
            "beta": bf(0.1 * np.random.standard_normal(D))}


def reference(lap, feat, w, gamma, beta):
    m = mxq(f64(lap), 1, "e4m3") @ mxq(f64(feat), 0, "e4m3")
    y = mxq(m, 1, "e4m3") @ mxq(f64(w), 1, "e4m3").T
    return leaky(layernorm(y, f64(gamma), f64(beta)))

@@ -1,0 +1,471 @@
+from contextlib import ExitStack
+
+import concourse.mybir as mybir
+from concourse.masks import make_identity
+
+F32 = mybir.dt.float32
+BF16 = mybir.dt.bfloat16
+U32 = mybir.dt.uint32
+U8 = mybir.dt.uint8
+FP8X4 = mybir.dt.float8_e4m3fn_x4
+ALU = mybir.AluOpType
+ACT = mybir.ActivationFunctionType
+
+P = 128
+N = 1024
+D = 1024
+NT = N // P
+EPS = 1e-5
+SLOPE = 0.1
+FLOPS = 2 * 2 * N * N * D
+MANUAL = True
+LAST_TILE = 7
+LAST_PIECES = 2
+
+ORDER = (
+    ("Lp", (0,), "PE"),
+    ("Wp", (0, 0,), "PE"),
+    ("Wp", (0, 1,), "PE"),
+    ("GBp", (0,), "PE"),
+    ("GBp", (1,), "PE"),
+    ("Wp", (1, 0,), "PE"),
+    ("Wp", (1, 1,), "PE"),
+    ("Wp", (2, 0,), "PE"),
+    ("Wp", (2, 1,), "PE"),
+    ("Wp", (3, 0,), "PE"),
+    ("Wp", (3, 1,), "PE"),
+    ("Lp", (1,), "PE"),
+    ("RG", (0, 0, 0,), "S"),
+    ("RG", (0, 0, 1,), "S"),
+    ("RG", (0, 1, 0,), "S"),
+    ("RG", (1, 0, 1,), "S"),
+    ("Ls", (0,), "S"),
+    ("Ws", (0, 0,), "S"),
+    ("Ws", (0, 1,), "S"),
+    ("Ws", (1, 0,), "S"),
+    ("Ws", (1, 1,), "S"),
+    ("Ws", (2, 0,), "S"),
+    ("Ws", (3, 0,), "S"),
+    ("Ws", (3, 1,), "S"),
+    ("Ls", (1,), "S"),
+    ("RG", (0, 1, 1,), "V"),
+    ("FQ", (0, 0,), "V"),
+    ("FQ", (0, 1,), "V"),
+    ("RG", (1, 0, 0,), "V"),
+    ("RG", (1, 1, 0,), "V"),
+    ("RG", (1, 1, 1,), "V"),
+    ("FQ", (1, 0,), "V"),
+    ("FQ", (1, 1,), "V"),
+    ("Lv", (0,), "V"),
+    ("Wv", (0, 0,), "V"),
+    ("Wv", (0, 1,), "V"),
+    ("Ws", (2, 1,), "V"),
+    ("Wv", (1, 0,), "V"),
+    ("Wv", (1, 1,), "V"),
+    ("Lv", (1,), "V"),
+    ("M1p", (0, 0,), "PE"),
+    ("M1p", (0, 1,), "PE"),
+    ("Lp", (2,), "PE"),
+    ("M1p", (1, 0,), "PE"),
+    ("M1p", (1, 1,), "PE"),
+    ("M1s", (0, 0,), "S"),
+    ("M1s", (0, 1,), "S"),
+    ("Ls", (2,), "S"),
+    ("M1s", (1, 0,), "S"),
+    ("M1v", (0,), "V"),
+    ("M1s", (1, 1,), "V"),
+    ("Lv", (2,), "V"),
+    ("M1v", (1,), "V"),
+    ("M2p", (0, 0,), "PE"),
+    ("M2p", (0, 1,), "PE"),
+    ("Lp", (3,), "PE"),
+    ("M1p", (2, 0,), "PE"),
+    ("M1p", (2, 1,), "PE"),
+    ("M2p", (1, 0,), "PE"),
+    ("M2p", (1, 1,), "PE"),
+    ("Lp", (4,), "PE"),
+    ("S1", (0, 0,), "S"),
+    ("S1", (0, 1,), "S"),
+    ("Ls", (3,), "S"),
+    ("NM", (0,), "V"),
+    ("M1s", (2, 0,), "V"),
+    ("M1s", (2, 1,), "V"),
+    ("Lv", (3,), "V"),
+    ("A", (0,), "V"),
+    ("M1v", (2,), "V"),
+    ("M1p", (3, 0,), "PE"),
+    ("M1p", (3, 1,), "PE"),
+    ("M2p", (2, 0,), "PE"),
+    ("M2p", (2, 1,), "PE"),
+    ("Lp", (5,), "PE"),
+    ("S2", (0,), "S"),
+    ("S1", (1, 0,), "S"),
+    ("S1", (1, 1,), "S"),
+    ("SQ", (0,), "S"),
+    ("Ls", (4,), "S"),
+    ("M1s", (3, 0,), "S"),
+    ("M1s", (3, 1,), "S"),
+    ("NM", (1,), "V"),
+    ("B", (0,), "V"),
+    ("Lv", (4,), "V"),
+    ("A", (1,), "V"),
+    ("M1v", (3,), "V"),
+    ("C", (0,), "V"),
+    ("M1p", (4, 0,), "PE"),
+    ("M1p", (4, 1,), "PE"),
+    ("M2p", (3, 0,), "PE"),
+    ("M2p", (3, 1,), "PE"),
+    ("Lp", (6,), "PE"),
+    ("S2", (1,), "S"),
+    ("S1", (2, 0,), "S"),
+    ("S1", (2, 1,), "S"),
+    ("SQ", (1,), "S"),
+    ("Ls", (5,), "S"),
+    ("M1s", (4, 0,), "S"),
+    ("NM", (2,), "V"),
+    ("M1s", (4, 1,), "V"),
+    ("B", (1,), "V"),
+    ("Lv", (5,), "V"),
+    ("A", (2,), "V"),
+    ("M1v", (4,), "V"),
+    ("C", (1,), "V"),
+    ("M1p", (5, 0,), "PE"),
+    ("M1p", (5, 1,), "PE"),
+    ("M2p", (4, 0,), "PE"),
+    ("M2p", (4, 1,), "PE"),
+    ("Lp", (7,), "PE"),
+    ("S2", (2,), "S"),
+    ("S1", (3, 0,), "S"),
+    ("S1", (3, 1,), "S"),
+    ("SQ", (2,), "S"),
+    ("Ls", (6,), "S"),
+    ("M1s", (5, 0,), "S"),
+    ("M1s", (5, 1,), "S"),
+    ("NM", (3,), "V"),
+    ("B", (2,), "V"),
+    ("Lv", (6,), "V"),
+    ("A", (3,), "V"),
+    ("M1v", (5,), "V"),
+    ("C", (2,), "V"),
+    ("M1p", (6, 0,), "PE"),
+    ("M1p", (6, 1,), "PE"),
+    ("M2p", (5, 0,), "PE"),
+    ("M2p", (5, 1,), "PE"),
+    ("S2", (3,), "S"),
+    ("S1", (4, 0,), "S"),
+    ("S1", (4, 1,), "S"),
+    ("SQ", (3,), "S"),
+    ("Ls", (7,), "S"),
+    ("M1s", (6, 0,), "S"),
+    ("M1s", (6, 1,), "S"),
+    ("NM", (4,), "V"),
+    ("B", (3,), "V"),
+    ("Lv", (7,), "V"),
+    ("A", (4,), "V"),
+    ("M1v", (6,), "V"),
+    ("C", (3,), "V"),
+    ("M1p", (7, 0,), "PE"),
+    ("M1p", (7, 1,), "PE"),
+    ("M2p", (6, 0,), "PE"),
+    ("M2p", (6, 1,), "PE"),
+    ("S2", (4,), "S"),
+    ("S1", (5, 0,), "S"),
+    ("S1", (5, 1,), "S"),
+    ("SQ", (4,), "S"),
+    ("M1s", (7, 0,), "S"),
+    ("M1s", (7, 1,), "S"),
+    ("NM", (5,), "V"),
+    ("B", (4,), "V"),
+    ("A", (5,), "V"),
+    ("M1v", (7,), "V"),
+    ("C", (4,), "V"),
+    ("M2p", (7, 0,), "PE"),
+    ("M2p", (7, 1,), "PE"),
+    ("S2", (5,), "S"),
+    ("S1", (6, 0,), "S"),
+    ("S1", (6, 1,), "S"),
+    ("SQ", (5,), "S"),
+    ("NM", (6,), "V"),
+    ("B", (5,), "V"),
+    ("A", (6,), "V"),
+    ("C", (5,), "V"),
+    ("S2", (6,), "S"),
+    ("S1", (7, 0,), "S"),
+    ("S1", (7, 1,), "S"),
+    ("SQ", (6,), "S"),
+    ("NM", (7,), "V"),
+    ("B", (6,), "V"),
+    ("A", (7,), "V"),
+    ("C", (6,), "V"),
+    ("S2", (7,), "S"),
+    ("SQ", (7,), "S"),
+    ("B", (7,), "V"),
+    ("C", (7,), "V"),
+)
+
+
+def tile_gcn_pb_kernel(tc, lap, feat, w, gamma, beta, out):
+    nc = tc.nc
+    with ExitStack() as ctx:
+        keep = ctx.enter_context(tc.tile_pool(name="keep", bufs=1))
+        ypool = ctx.enter_context(tc.tile_pool(name="ypool", bufs=4))
+        opool = ctx.enter_context(tc.tile_pool(name="opool", bufs=4))
+        small = ctx.enter_context(tc.tile_pool(name="small", bufs=6))
+        psum = ctx.enter_context(tc.psum_pool(name="psum", bufs=6))
+        if MANUAL:
+            ctx.enter_context(tc.manual_schedule())
+
+        gb_row = keep.tile([P, 2 * D], BF16)
+        nc.vector.memset(gb_row[:], 0.0)
+        nc.scalar.dma_start(out=gb_row[0:1, 0:D], in_=gamma.rearrange("(o d) -> o d", o=1))
+        nc.scalar.dma_start(out=gb_row[0:1, D : 2 * D], in_=beta.rearrange("(o d) -> o d", o=1))
+        eps_t = keep.tile([P, 1], F32)
+        nc.vector.memset(eps_t[:], EPS)
+        warm = keep.tile([P, 1], F32)
+        nc.scalar.activation(out=warm[:], in_=eps_t[:], func=ACT.Abs_reciprocal_sqrt)
+        ident = keep.tile([P, P], F32)
+        make_identity(nc, ident[:])
+        ones = keep.tile([P, P], BF16)
+        nc.vector.memset(ones[:], 1.0)
+
+        fr = keep.tile([P, 2, 4, D], BF16)
+        lap_sb = keep.tile([P, NT, N], BF16)
+        w_sb = keep.tile([P, NT, D], BF16)
+        lap_v = lap.rearrange("(p t) j -> p t j", t=NT)
+
+        def load_w(k):
+            nc.sync.dma_start(
+                out=w_sb[:, 2 * k : 2 * k + 2, :],
+                in_=w[256 * k : 256 * k + 256, :].rearrange("(t p) d -> p t d", p=P),
+            )
+
+        def load_f(g, u):
+            rows = feat[512 * g : 512 * g + 512, :].rearrange("(q t) c -> q t c", t=4)
+            nc.sync.dma_start(out=fr[:, g, 2 * u : 2 * u + 2, :], in_=rows[:, 2 * u : 2 * u + 2, :])
+
+        def load_l(t0, t1):
+            nc.sync.dma_start(out=lap_sb[:, t0:t1, :], in_=lap_v[:, t0:t1, :])
+
+        load_f(0, 0)
+        load_f(0, 1)
+        load_l(0, 2)
+        load_f(1, 0)
+        load_f(1, 1)
+        load_w(0)
+        load_w(1)
+        load_w(2)
+        load_w(3)
+        load_l(2, 4)
+        load_l(4, 8)
+        lap_w = lap_sb[:].bitcast(F32)
+        w_w = w_sb[:].bitcast(F32)
+
+        fg = keep.tile([P, 2, D, 4], BF16, align_bytes=64)
+        f_codes = keep.tile([P, 2, D], U32, align_bytes=64)
+        f_sc = keep.tile([P, 2, D], U8, align_bytes=64)
+        lg = keep.tile([P, NT, 2, P, 4], BF16, align_bytes=64)
+        lg_w = lg[:].bitcast(F32)
+        l_codes = keep.tile([P, NT, 2, P], U32, align_bytes=64)
+        l_sc = keep.tile([P, NT, 2, P], U8, align_bytes=64)
+        wg = keep.tile([P, 2, D, 4], BF16, align_bytes=64)
+        wg_w = wg[:].bitcast(F32)
+        w_codes = keep.tile([P, 2, D], U32, align_bytes=64)
+        w_sc = keep.tile([P, 2, D], U8, align_bytes=64)
+        mg = keep.tile([P, NT, 2, P, 4], BF16, align_bytes=64)
+        m_codes = keep.tile([P, NT, 2, P], U32, align_bytes=64)
+        m_sc = keep.tile([P, NT, 2, P], U8, align_bytes=64)
+        out_v = out.rearrange("(p t) o -> p t o", t=NT)
+        live = {}
+
+        def copy_on(eng, dst, src):
+            if eng == "V":
+                nc.vector.tensor_copy(out=dst, in_=src)
+            else:
+                nc.scalar.copy(out=dst, in_=src)
+
+        def op_GBp(a, eng):
+            k = a[0]
+            bank = psum.tile([P, D], BF16, name="gb%d" % k, tag="gb%d" % k, bufs=1)
+            for h in range(2):
+                c0 = D * k + 512 * h
+                nc.tensor.matmul(
+                    out=bank[:, 512 * h : 512 * h + 512], lhsT=ones[:], rhs=gb_row[:, c0 : c0 + 512], start=True, stop=True
+                )
+            live[("gb", k)] = bank
+
+        def op_RG(a, eng):
+            g, g2, u = a
+            c0 = 512 * g2 + 256 * u
+            src = fr[:, g, :, c0 : c0 + 256].rearrange("p t (c i s) -> p s c t i", i=2, s=4)
+            dst = fg[:, g, 512 * g2 : 512 * g2 + 512, :].rearrange("p (s m) t -> p s m t", s=4)
+            dst = dst[:, :, 64 * u : 64 * u + 64, :].rearrange("p s (c i) t -> p s c t i", i=2)
+            if eng == "V":
+                nc.vector.tensor_copy(out=dst, in_=src)
+            else:
+                for s in range(4):
+                    nc.scalar.copy(out=dst[:, s], in_=src[:, s])
+
+        def op_FQ(a, eng):
+            g, g2 = a
+            cs = slice(512 * g2, 512 * g2 + 512)
+            nc.vector.quantize_mx(
+                out=f_codes[:, g, cs].bitcast(FP8X4),
+                scales=f_sc[:, g, cs],
+                in_=fg[:, g, cs, :].rearrange("p c t -> p (c t)"),
+            )
+
+        def op_Lp(a, eng):
+            it = a[0]
+            tp = psum.tile([P, 2, 2, P], F32, name="tp", tag="ps")
+            for g in range(2):
+                for u in range(2):
+                    nc.tensor.transpose(tp[:, g, u, :], lap_w[:, it, 256 * g + u : 256 * g + 256 : 2], ident[:])
+            live[("L", it)] = tp
+
+        def op_Ls(a, eng):
+            it = a[0]
+            copy_on(eng, lg_w[:, it], live[("L", it)][:].rearrange("p g u i -> p g i u"))
+
+        def op_Lv(a, eng):
+            it = a[0]
+            nc.vector.quantize_mx(
+                out=l_codes[:, it].rearrange("p g i -> p (g i)").bitcast(FP8X4),
+                scales=l_sc[:, it].rearrange("p g i -> p (g i)"),
+                in_=lg[:, it].rearrange("p g i t -> p (g i t)"),
+            )
+
+        def op_Wp(a, eng):
+            pr, g2 = a
+            tp = psum.tile([P, 2, 2, P], F32, name="tp", tag="ps")
+            for b in range(2):
+                for u in range(2):
+                    words = w_w[:, 2 * pr + b, 256 * g2 + u : 256 * g2 + 256 : 2]
+                    nc.tensor.transpose(tp[:, u, b, :], words, ident[:])
+            live[("W", pr, g2)] = tp
+
+        def op_Ws(a, eng):
+            pr, g2 = a
+            copy_on(eng, wg_w[:, g2, 256 * pr : 256 * pr + 256, :], live[("W", pr, g2)][:].rearrange("p u b o -> p (b o) u"))
+
+        def op_Wv(a, eng):
+            h, g2 = a
+            cs = slice(512 * h, 512 * h + 512)
+            nc.vector.quantize_mx(
+                out=w_codes[:, g2, cs].bitcast(FP8X4),
+                scales=w_sc[:, g2, cs],
+                in_=wg[:, g2, cs, :].rearrange("p c t -> p (c t)"),
+            )
+
+        def op_M1p(a, eng):
+            it, g2 = a
+            mp = psum.tile([P, 4, P], F32, name="mp", tag="ps")
+            for t2 in range(4):
+                cs = slice((4 * g2 + t2) * P, (4 * g2 + t2 + 1) * P)
+                for g in range(2):
+                    nc.tensor.matmul_mx(
+                        out=mp[:, t2, :],
+                        lhsT=f_codes[:, g, cs].bitcast(FP8X4),
+                        lhsT_scale=f_sc[:, g, cs],
+                        rhs=l_codes[:, it, g, :].bitcast(FP8X4),
+                        rhs_scale=l_sc[:, it, g, :],
+                        start=(g == 0),
+                        stop=(g == 1),
+                    )
+            live[("M", it, g2)] = mp
+
+        def op_M1s(a, eng):
+            it, g2 = a
+            copy_on(eng, mg[:, it, g2], live[("M", it, g2)][:].rearrange("p t i -> p i t"))
+
+        def op_M1v(a, eng):
+            it = a[0]
+            nc.vector.quantize_mx(
+                out=m_codes[:, it].rearrange("p g i -> p (g i)").bitcast(FP8X4),
+                scales=m_sc[:, it].rearrange("p g i -> p (g i)"),
+                in_=mg[:, it].rearrange("p g i t -> p (g i t)"),
+            )
+
+        def op_M2p(a, eng):
+            it, h = a
+            yp = psum.tile([P, 512], F32, name="yp", tag="ps")
+            cs = slice(512 * h, 512 * h + 512)
+            for g2 in range(2):
+                nc.tensor.matmul_mx(
+                    out=yp[:],
+                    lhsT=m_codes[:, it, g2, :].bitcast(FP8X4),
+                    lhsT_scale=m_sc[:, it, g2, :],
+                    rhs=w_codes[:, g2, cs].bitcast(FP8X4),
+                    rhs_scale=w_sc[:, g2, cs],
+                    start=(g2 == 0),
+                    stop=(g2 == 1),
+                )
+            live[("Y", it, h)] = yp
+
+        def op_S1(a, eng):
+            it, h = a
+            if h == 0:
+                live[("ysb", it)] = ypool.tile([P, D], F32, name="y_sb", tag="y_sb")
+                live[("sums", it)] = small.tile([P, 2], F32, name="sums", tag="sums")
+            cs = slice(512 * h, 512 * h + 512)
+            nc.scalar.activation(
+                out=live[("ysb", it)][:, cs], in_=live[("Y", it, h)][:], func=ACT.Copy, accum_out=live[("sums", it)][:, h : h + 1]
+            )
+
+        def op_NM(a, eng):
+            it = a[0]
+            negmu = small.tile([P, 1], F32, name="negmu", tag="negmu")
+            sums = live[("sums", it)]
+            nc.vector.tensor_scalar(
+                out=negmu[:], in0=sums[:, 0:1], scalar1=sums[:, 1:2], scalar2=-1.0 / D, op0=ALU.add, op1=ALU.mult
+            )
+            live[("negmu", it)] = negmu
+
+        def op_S2(a, eng):
+            it = a[0]
+            ssq = small.tile([P, 1], F32, name="ssq", tag="ssq")
+            junk = keep.tile([P, D], BF16, name="junk", tag="junk")
+            nc.scalar.activation(
+                out=junk[:], in_=live[("ysb", it)][:], func=ACT.Square, bias=live[("negmu", it)][:, 0:1], scale=1.0, accum_out=ssq[:]
+            )
+            live[("ssq", it)] = ssq
+
+        def op_SQ(a, eng):
+            it = a[0]
+            rstd = small.tile([P, 1], F32, name="rstd", tag="rstd")
+            nc.scalar.activation(
+                out=rstd[:], in_=live[("ssq", it)][:], func=ACT.Abs_reciprocal_sqrt, bias=eps_t[:, 0:1], scale=1.0 / D
+            )
+            live[("rstd", it)] = rstd
+
+        def op_A(a, eng):
+            it = a[0]
+            z = opool.tile([P, D], F32, name="z", tag="z")
+            nc.vector.scalar_tensor_tensor(
+                out=z[:], in0=live[("ysb", it)][:], scalar=live[("negmu", it)][:, 0:1], in1=live[("gb", 0)][:], op0=ALU.add, op1=ALU.mult
+            )
+            live[("z", it)] = z
+
+        def op_B(a, eng):
+            it = a[0]
+            z = live[("z", it)]
+            nc.vector.scalar_tensor_tensor(
+                out=z[:], in0=z[:], scalar=live[("rstd", it)][:, 0:1], in1=live[("gb", 1)][:], op0=ALU.mult, op1=ALU.add
+            )
+
+        def op_C(a, eng):
+            it = a[0]
+            z = live[("z", it)]
+            pieces = LAST_PIECES if it == LAST_TILE else 1
+            width = D // pieces
+            for c in range(pieces):
+                cs = slice(c * width, (c + 1) * width)
+                nc.vector.scalar_tensor_tensor(out=z[:, cs], in0=z[:, cs], scalar=SLOPE, in1=z[:, cs], op0=ALU.mult, op1=ALU.max)
+                nc.sync.dma_start(out=out_v[:, it, cs], in_=z[:, cs])
+
+        table = {
+            "GBp": op_GBp, "RG": op_RG, "FQ": op_FQ, "Lp": op_Lp, "Ls": op_Ls, "Lv": op_Lv, "Wp": op_Wp, "Ws": op_Ws,
+            "Wv": op_Wv, "M1p": op_M1p, "M1s": op_M1s, "M1v": op_M1v, "M2p": op_M2p, "S1": op_S1, "NM": op_NM,
+            "S2": op_S2, "SQ": op_SQ, "A": op_A, "B": op_B, "C": op_C,
+        }
+        for kind, args, eng in ORDER:
+            table[kind](args, eng)

@@ -18,220 +18,42 @@ NT = N // P
 EPS = 1e-5
 SLOPE = 0.1
 FLOPS = 2 * 2 * N * N * D
-MANUAL = True
-LAST_TILE = 7
-LAST_PIECES = 2
-
-ORDER = (
-    ("Lp", (0,), "PE"),
-    ("Wp", (0, 0,), "PE"),
-    ("Wp", (0, 1,), "PE"),
-    ("GBp", (0,), "PE"),
-    ("GBp", (1,), "PE"),
-    ("Wp", (1, 0,), "PE"),
-    ("Wp", (1, 1,), "PE"),
-    ("Wp", (2, 0,), "PE"),
-    ("Wp", (2, 1,), "PE"),
-    ("Wp", (3, 0,), "PE"),
-    ("Wp", (3, 1,), "PE"),
-    ("Lp", (1,), "PE"),
-    ("RG", (0, 0, 0,), "S"),
-    ("RG", (0, 0, 1,), "S"),
-    ("RG", (0, 1, 0,), "S"),
-    ("RG", (1, 0, 1,), "S"),
-    ("Ls", (0,), "S"),
-    ("Ws", (0, 0,), "S"),
-    ("Ws", (0, 1,), "S"),
-    ("Ws", (1, 0,), "S"),
-    ("Ws", (1, 1,), "S"),
-    ("Ws", (2, 0,), "S"),
-    ("Ws", (3, 0,), "S"),
-    ("Ws", (3, 1,), "S"),
-    ("Ls", (1,), "S"),
-    ("RG", (0, 1, 1,), "V"),
-    ("FQ", (0, 0,), "V"),
-    ("FQ", (0, 1,), "V"),
-    ("RG", (1, 0, 0,), "V"),
-    ("RG", (1, 1, 0,), "V"),
-    ("RG", (1, 1, 1,), "V"),
-    ("FQ", (1, 0,), "V"),
-    ("FQ", (1, 1,), "V"),
-    ("Lv", (0,), "V"),
-    ("Wv", (0, 0,), "V"),
-    ("Wv", (0, 1,), "V"),
-    ("Ws", (2, 1,), "V"),
-    ("Wv", (1, 0,), "V"),
-    ("Wv", (1, 1,), "V"),
-    ("Lv", (1,), "V"),
-    ("M1p", (0, 0,), "PE"),
-    ("M1p", (0, 1,), "PE"),
-    ("Lp", (2,), "PE"),
-    ("M1p", (1, 0,), "PE"),
-    ("M1p", (1, 1,), "PE"),
-    ("M1s", (0, 0,), "S"),
-    ("M1s", (0, 1,), "S"),
-    ("Ls", (2,), "S"),
-    ("M1s", (1, 0,), "S"),
-    ("M1v", (0,), "V"),
-    ("M1s", (1, 1,), "V"),
-    ("Lv", (2,), "V"),
-    ("M1v", (1,), "V"),
-    ("M2p", (0, 0,), "PE"),
-    ("M2p", (0, 1,), "PE"),
-    ("Lp", (3,), "PE"),
-    ("M1p", (2, 0,), "PE"),
-    ("M1p", (2, 1,), "PE"),
-    ("M2p", (1, 0,), "PE"),
-    ("M2p", (1, 1,), "PE"),
-    ("Lp", (4,), "PE"),
-    ("S1", (0, 0,), "S"),
-    ("S1", (0, 1,), "S"),
-    ("Ls", (3,), "S"),
-    ("NM", (0,), "V"),
-    ("M1s", (2, 0,), "V"),
-    ("M1s", (2, 1,), "V"),
-    ("Lv", (3,), "V"),
-    ("A", (0,), "V"),
-    ("M1v", (2,), "V"),
-    ("M1p", (3, 0,), "PE"),
-    ("M1p", (3, 1,), "PE"),
-    ("M2p", (2, 0,), "PE"),
-    ("M2p", (2, 1,), "PE"),
-    ("Lp", (5,), "PE"),
-    ("S2", (0,), "S"),
-    ("S1", (1, 0,), "S"),
-    ("S1", (1, 1,), "S"),
-    ("SQ", (0,), "S"),
-    ("Ls", (4,), "S"),
-    ("M1s", (3, 0,), "S"),
-    ("M1s", (3, 1,), "S"),
-    ("NM", (1,), "V"),
-    ("B", (0,), "V"),
-    ("Lv", (4,), "V"),
-    ("A", (1,), "V"),
-    ("M1v", (3,), "V"),
-    ("C", (0,), "V"),
-    ("M1p", (4, 0,), "PE"),
-    ("M1p", (4, 1,), "PE"),
-    ("M2p", (3, 0,), "PE"),
-    ("M2p", (3, 1,), "PE"),
-    ("Lp", (6,), "PE"),
-    ("S2", (1,), "S"),
-    ("S1", (2, 0,), "S"),
-    ("S1", (2, 1,), "S"),
-    ("SQ", (1,), "S"),
-    ("Ls", (5,), "S"),
-    ("M1s", (4, 0,), "S"),
-    ("NM", (2,), "V"),
-    ("M1s", (4, 1,), "V"),
-    ("B", (1,), "V"),
-    ("Lv", (5,), "V"),
-    ("A", (2,), "V"),
-    ("M1v", (4,), "V"),
-    ("C", (1,), "V"),
-    ("M1p", (5, 0,), "PE"),
-    ("M1p", (5, 1,), "PE"),
-    ("M2p", (4, 0,), "PE"),
-    ("M2p", (4, 1,), "PE"),
-    ("Lp", (7,), "PE"),
-    ("S2", (2,), "S"),
-    ("S1", (3, 0,), "S"),
-    ("S1", (3, 1,), "S"),
-    ("SQ", (2,), "S"),
-    ("Ls", (6,), "S"),
-    ("M1s", (5, 0,), "S"),
-    ("M1s", (5, 1,), "S"),
-    ("NM", (3,), "V"),
-    ("B", (2,), "V"),
-    ("Lv", (6,), "V"),
-    ("A", (3,), "V"),
-    ("M1v", (5,), "V"),
-    ("C", (2,), "V"),
-    ("M1p", (6, 0,), "PE"),
-    ("M1p", (6, 1,), "PE"),
-    ("M2p", (5, 0,), "PE"),
-    ("M2p", (5, 1,), "PE"),
-    ("S2", (3,), "S"),
-    ("S1", (4, 0,), "S"),
-    ("S1", (4, 1,), "S"),
-    ("SQ", (3,), "S"),
-    ("Ls", (7,), "S"),
-    ("M1s", (6, 0,), "S"),
-    ("M1s", (6, 1,), "S"),
-    ("NM", (4,), "V"),
-    ("B", (3,), "V"),
-    ("Lv", (7,), "V"),
-    ("A", (4,), "V"),
-    ("M1v", (6,), "V"),
-    ("C", (3,), "V"),
-    ("M1p", (7, 0,), "PE"),
-    ("M1p", (7, 1,), "PE"),
-    ("M2p", (6, 0,), "PE"),
-    ("M2p", (6, 1,), "PE"),
-    ("S2", (4,), "S"),
-    ("S1", (5, 0,), "S"),
-    ("S1", (5, 1,), "S"),
-    ("SQ", (4,), "S"),
-    ("M1s", (7, 0,), "S"),
-    ("M1s", (7, 1,), "S"),
-    ("NM", (5,), "V"),
-    ("B", (4,), "V"),
-    ("A", (5,), "V"),
-    ("M1v", (7,), "V"),
-    ("C", (4,), "V"),
-    ("M2p", (7, 0,), "PE"),
-    ("M2p", (7, 1,), "PE"),
-    ("S2", (5,), "S"),
-    ("S1", (6, 0,), "S"),
-    ("S1", (6, 1,), "S"),
-    ("SQ", (5,), "S"),
-    ("NM", (6,), "V"),
-    ("B", (5,), "V"),
-    ("A", (6,), "V"),
-    ("C", (5,), "V"),
-    ("S2", (6,), "S"),
-    ("S1", (7, 0,), "S"),
-    ("S1", (7, 1,), "S"),
-    ("SQ", (6,), "S"),
-    ("NM", (7,), "V"),
-    ("B", (6,), "V"),
-    ("A", (7,), "V"),
-    ("C", (6,), "V"),
-    ("S2", (7,), "S"),
-    ("SQ", (7,), "S"),
-    ("B", (7,), "V"),
-    ("C", (7,), "V"),
-)
 
 
 def tile_gcn_pb_kernel(tc, lap, feat, w, gamma, beta, out):
     nc = tc.nc
+    V, S = nc.vector, nc.scalar
     with ExitStack() as ctx:
         keep = ctx.enter_context(tc.tile_pool(name="keep", bufs=1))
         ypool = ctx.enter_context(tc.tile_pool(name="ypool", bufs=4))
         opool = ctx.enter_context(tc.tile_pool(name="opool", bufs=4))
         small = ctx.enter_context(tc.tile_pool(name="small", bufs=6))
         psum = ctx.enter_context(tc.psum_pool(name="psum", bufs=6))
-        if MANUAL:
-            ctx.enter_context(tc.manual_schedule())
+        ctx.enter_context(tc.manual_schedule())
 
         gb_row = keep.tile([P, 2 * D], BF16)
-        nc.vector.memset(gb_row[:], 0.0)
-        nc.scalar.dma_start(out=gb_row[0:1, 0:D], in_=gamma.rearrange("(o d) -> o d", o=1))
-        nc.scalar.dma_start(out=gb_row[0:1, D : 2 * D], in_=beta.rearrange("(o d) -> o d", o=1))
+        V.memset(gb_row[:, 0:D], 0.0)
+        nc.gpsimd.memset(gb_row[:, D : 2 * D], 0.0)
         eps_t = keep.tile([P, 1], F32)
-        nc.vector.memset(eps_t[:], EPS)
+        V.memset(eps_t[:], EPS)
         warm = keep.tile([P, 1], F32)
-        nc.scalar.activation(out=warm[:], in_=eps_t[:], func=ACT.Abs_reciprocal_sqrt)
+        S.activation(out=warm[:], in_=eps_t[:], func=ACT.Abs_reciprocal_sqrt)
         ident = keep.tile([P, P], F32)
         make_identity(nc, ident[:])
         ones = keep.tile([P, P], BF16)
-        nc.vector.memset(ones[:], 1.0)
+        V.memset(ones[:], 1.0)
 
-        fr = keep.tile([P, 2, 4, D], BF16)
+        fr = keep.tile([P, 2, 2, 4, 512], BF16)
         lap_sb = keep.tile([P, NT, N], BF16)
         w_sb = keep.tile([P, NT, D], BF16)
         lap_v = lap.rearrange("(p t) j -> p t j", t=NT)
+
+        def load_f(g, g2):
+            rows = feat[512 * g : 512 * g + 512, :].rearrange("(q t) c -> q t c", t=4)
+            nc.sync.dma_start(out=fr[:, g, g2], in_=rows[:, :, 512 * g2 : 512 * g2 + 512])
+
+        def load_gb(k, vec):
+            nc.sync.dma_start(out=gb_row[0:1, D * k : D * k + D], in_=vec.rearrange("(o d) -> o d", o=1))
 
         def load_w(k):
             nc.sync.dma_start(
@@ -239,20 +61,19 @@ def tile_gcn_pb_kernel(tc, lap, feat, w, gamma, beta, out):
                 in_=w[256 * k : 256 * k + 256, :].rearrange("(t p) d -> p t d", p=P),
             )
 
-        def load_f(g, u):
-            rows = feat[512 * g : 512 * g + 512, :].rearrange("(q t) c -> q t c", t=4)
-            nc.sync.dma_start(out=fr[:, g, 2 * u : 2 * u + 2, :], in_=rows[:, 2 * u : 2 * u + 2, :])
-
         def load_l(t0, t1):
             nc.sync.dma_start(out=lap_sb[:, t0:t1, :], in_=lap_v[:, t0:t1, :])
 
         load_f(0, 0)
         load_f(0, 1)
-        load_l(0, 2)
+        load_gb(0, gamma)
+        load_gb(1, beta)
         load_f(1, 0)
         load_f(1, 1)
+        load_l(0, 1)
         load_w(0)
         load_w(1)
+        load_l(1, 2)
         load_w(2)
         load_w(3)
         load_l(2, 4)
@@ -278,115 +99,100 @@ def tile_gcn_pb_kernel(tc, lap, feat, w, gamma, beta, out):
         live = {}
 
         def copy_on(eng, dst, src):
-            if eng == "V":
-                nc.vector.tensor_copy(out=dst, in_=src)
+            if eng is V:
+                V.tensor_copy(out=dst, in_=src)
             else:
-                nc.scalar.copy(out=dst, in_=src)
+                S.copy(out=dst, in_=src)
 
-        def op_GBp(a, eng):
-            k = a[0]
-            bank = psum.tile([P, D], BF16, name="gb%d" % k, tag="gb%d" % k, bufs=1)
-            for h in range(2):
-                c0 = D * k + 512 * h
-                nc.tensor.matmul(
-                    out=bank[:, 512 * h : 512 * h + 512], lhsT=ones[:], rhs=gb_row[:, c0 : c0 + 512], start=True, stop=True
-                )
-            live[("gb", k)] = bank
+        def gb_broadcast():
+            for k in range(2):
+                bank = psum.tile([P, D], BF16, name="gb%d" % k, tag="gb%d" % k, bufs=1)
+                for h in range(2):
+                    c0 = D * k + 512 * h
+                    nc.tensor.matmul(
+                        out=bank[:, 512 * h : 512 * h + 512], lhsT=ones[:], rhs=gb_row[:, c0 : c0 + 512], start=True, stop=True
+                    )
+                live[("gb", k)] = bank
 
-        def op_RG(a, eng):
-            g, g2, u = a
-            c0 = 512 * g2 + 256 * u
-            src = fr[:, g, :, c0 : c0 + 256].rearrange("p t (c i s) -> p s c t i", i=2, s=4)
-            dst = fg[:, g, 512 * g2 : 512 * g2 + 512, :].rearrange("p (s m) t -> p s m t", s=4)
-            dst = dst[:, :, 64 * u : 64 * u + 64, :].rearrange("p s (c i) t -> p s c t i", i=2)
-            if eng == "V":
-                nc.vector.tensor_copy(out=dst, in_=src)
+        def f_group(eng, g, g2, s0, s1):
+            src = fr[:, g, g2].rearrange("p t (c i s) -> p s c t i", i=2, s=4)
+            dst = fg[:, g, 512 * g2 : 512 * g2 + 512, :].rearrange("p (s c i) t -> p s c t i", s=4, i=2)
+            if eng is V:
+                V.tensor_copy(out=dst[:, s0:s1], in_=src[:, s0:s1])
             else:
-                for s in range(4):
-                    nc.scalar.copy(out=dst[:, s], in_=src[:, s])
+                for s in range(s0, s1):
+                    S.copy(out=dst[:, s], in_=src[:, s])
 
-        def op_FQ(a, eng):
-            g, g2 = a
+        def f_quant(g, g2):
             cs = slice(512 * g2, 512 * g2 + 512)
-            nc.vector.quantize_mx(
-                out=f_codes[:, g, cs].bitcast(FP8X4),
-                scales=f_sc[:, g, cs],
-                in_=fg[:, g, cs, :].rearrange("p c t -> p (c t)"),
+            V.quantize_mx(
+                out=f_codes[:, g, cs].bitcast(FP8X4), scales=f_sc[:, g, cs], in_=fg[:, g, cs, :].rearrange("p c t -> p (c t)")
             )
 
-        def op_Lp(a, eng):
-            it = a[0]
+        def l_turn(it):
             tp = psum.tile([P, 2, 2, P], F32, name="tp", tag="ps")
             for g in range(2):
                 for u in range(2):
                     nc.tensor.transpose(tp[:, g, u, :], lap_w[:, it, 256 * g + u : 256 * g + 256 : 2], ident[:])
             live[("L", it)] = tp
 
-        def op_Ls(a, eng):
-            it = a[0]
+        def l_out(eng, it):
             copy_on(eng, lg_w[:, it], live[("L", it)][:].rearrange("p g u i -> p g i u"))
 
-        def op_Lv(a, eng):
-            it = a[0]
-            nc.vector.quantize_mx(
+        def l_quant(it):
+            V.quantize_mx(
                 out=l_codes[:, it].rearrange("p g i -> p (g i)").bitcast(FP8X4),
                 scales=l_sc[:, it].rearrange("p g i -> p (g i)"),
                 in_=lg[:, it].rearrange("p g i t -> p (g i t)"),
             )
 
-        def op_Wp(a, eng):
-            pr, g2 = a
-            tp = psum.tile([P, 2, 2, P], F32, name="tp", tag="ps")
-            for b in range(2):
-                for u in range(2):
-                    words = w_w[:, 2 * pr + b, 256 * g2 + u : 256 * g2 + 256 : 2]
-                    nc.tensor.transpose(tp[:, u, b, :], words, ident[:])
-            live[("W", pr, g2)] = tp
+        def w_turn(pr):
+            for g2 in range(2):
+                tp = psum.tile([P, 2, 2, P], F32, name="tp", tag="ps")
+                for b in range(2):
+                    for u in range(2):
+                        words = w_w[:, 2 * pr + b, 256 * g2 + u : 256 * g2 + 256 : 2]
+                        nc.tensor.transpose(tp[:, u, b, :], words, ident[:])
+                live[("W", pr, g2)] = tp
 
-        def op_Ws(a, eng):
-            pr, g2 = a
+        def w_out(eng, pr, g2):
             copy_on(eng, wg_w[:, g2, 256 * pr : 256 * pr + 256, :], live[("W", pr, g2)][:].rearrange("p u b o -> p (b o) u"))
 
-        def op_Wv(a, eng):
-            h, g2 = a
+        def w_quant(h):
             cs = slice(512 * h, 512 * h + 512)
-            nc.vector.quantize_mx(
-                out=w_codes[:, g2, cs].bitcast(FP8X4),
-                scales=w_sc[:, g2, cs],
-                in_=wg[:, g2, cs, :].rearrange("p c t -> p (c t)"),
-            )
+            for g2 in range(2):
+                V.quantize_mx(
+                    out=w_codes[:, g2, cs].bitcast(FP8X4), scales=w_sc[:, g2, cs], in_=wg[:, g2, cs, :].rearrange("p c t -> p (c t)")
+                )
 
-        def op_M1p(a, eng):
-            it, g2 = a
-            mp = psum.tile([P, 4, P], F32, name="mp", tag="ps")
-            for t2 in range(4):
-                cs = slice((4 * g2 + t2) * P, (4 * g2 + t2 + 1) * P)
-                for g in range(2):
-                    nc.tensor.matmul_mx(
-                        out=mp[:, t2, :],
-                        lhsT=f_codes[:, g, cs].bitcast(FP8X4),
-                        lhsT_scale=f_sc[:, g, cs],
-                        rhs=l_codes[:, it, g, :].bitcast(FP8X4),
-                        rhs_scale=l_sc[:, it, g, :],
-                        start=(g == 0),
-                        stop=(g == 1),
-                    )
-            live[("M", it, g2)] = mp
+        def m_mul(it):
+            for g2 in range(2):
+                mp = psum.tile([P, 4, P], F32, name="mp", tag="ps")
+                for t2 in range(4):
+                    cs = slice((4 * g2 + t2) * P, (4 * g2 + t2 + 1) * P)
+                    for g in range(2):
+                        nc.tensor.matmul_mx(
+                            out=mp[:, t2, :],
+                            lhsT=f_codes[:, g, cs].bitcast(FP8X4),
+                            lhsT_scale=f_sc[:, g, cs],
+                            rhs=l_codes[:, it, g, :].bitcast(FP8X4),
+                            rhs_scale=l_sc[:, it, g, :],
+                            start=(g == 0),
+                            stop=(g == 1),
+                        )
+                live[("M", it, g2)] = mp
 
-        def op_M1s(a, eng):
-            it, g2 = a
+        def m_out(eng, it, g2):
             copy_on(eng, mg[:, it, g2], live[("M", it, g2)][:].rearrange("p t i -> p i t"))
 
-        def op_M1v(a, eng):
-            it = a[0]
-            nc.vector.quantize_mx(
+        def m_quant(it):
+            V.quantize_mx(
                 out=m_codes[:, it].rearrange("p g i -> p (g i)").bitcast(FP8X4),
                 scales=m_sc[:, it].rearrange("p g i -> p (g i)"),
                 in_=mg[:, it].rearrange("p g i t -> p (g i t)"),
             )
 
-        def op_M2p(a, eng):
-            it, h = a
+        def y_mul(it, h):
             yp = psum.tile([P, 512], F32, name="yp", tag="ps")
             cs = slice(512 * h, 512 * h + 512)
             for g2 in range(2):
@@ -401,71 +207,137 @@ def tile_gcn_pb_kernel(tc, lap, feat, w, gamma, beta, out):
                 )
             live[("Y", it, h)] = yp
 
-        def op_S1(a, eng):
-            it, h = a
+        def y_out(it, h):
             if h == 0:
                 live[("ysb", it)] = ypool.tile([P, D], F32, name="y_sb", tag="y_sb")
                 live[("sums", it)] = small.tile([P, 2], F32, name="sums", tag="sums")
-            cs = slice(512 * h, 512 * h + 512)
-            nc.scalar.activation(
-                out=live[("ysb", it)][:, cs], in_=live[("Y", it, h)][:], func=ACT.Copy, accum_out=live[("sums", it)][:, h : h + 1]
+            S.activation(
+                out=live[("ysb", it)][:, 512 * h : 512 * h + 512],
+                in_=live[("Y", it, h)][:],
+                func=ACT.Copy,
+                accum_out=live[("sums", it)][:, h : h + 1],
             )
 
-        def op_NM(a, eng):
-            it = a[0]
+        def y_mean(it):
             negmu = small.tile([P, 1], F32, name="negmu", tag="negmu")
             sums = live[("sums", it)]
-            nc.vector.tensor_scalar(
-                out=negmu[:], in0=sums[:, 0:1], scalar1=sums[:, 1:2], scalar2=-1.0 / D, op0=ALU.add, op1=ALU.mult
-            )
+            V.tensor_scalar(out=negmu[:], in0=sums[:, 0:1], scalar1=sums[:, 1:2], scalar2=-1.0 / D, op0=ALU.add, op1=ALU.mult)
             live[("negmu", it)] = negmu
 
-        def op_S2(a, eng):
-            it = a[0]
+        def y_square(it):
             ssq = small.tile([P, 1], F32, name="ssq", tag="ssq")
             junk = keep.tile([P, D], BF16, name="junk", tag="junk")
-            nc.scalar.activation(
+            S.activation(
                 out=junk[:], in_=live[("ysb", it)][:], func=ACT.Square, bias=live[("negmu", it)][:, 0:1], scale=1.0, accum_out=ssq[:]
             )
             live[("ssq", it)] = ssq
 
-        def op_SQ(a, eng):
-            it = a[0]
+        def y_rstd(it):
             rstd = small.tile([P, 1], F32, name="rstd", tag="rstd")
-            nc.scalar.activation(
-                out=rstd[:], in_=live[("ssq", it)][:], func=ACT.Abs_reciprocal_sqrt, bias=eps_t[:, 0:1], scale=1.0 / D
-            )
+            S.activation(out=rstd[:], in_=live[("ssq", it)][:], func=ACT.Abs_reciprocal_sqrt, bias=eps_t[:, 0:1], scale=1.0 / D)
             live[("rstd", it)] = rstd
 
-        def op_A(a, eng):
-            it = a[0]
+        def z_gamma(it):
             z = opool.tile([P, D], F32, name="z", tag="z")
-            nc.vector.scalar_tensor_tensor(
+            V.scalar_tensor_tensor(
                 out=z[:], in0=live[("ysb", it)][:], scalar=live[("negmu", it)][:, 0:1], in1=live[("gb", 0)][:], op0=ALU.add, op1=ALU.mult
             )
             live[("z", it)] = z
 
-        def op_B(a, eng):
-            it = a[0]
+        def z_beta(it):
             z = live[("z", it)]
-            nc.vector.scalar_tensor_tensor(
+            V.scalar_tensor_tensor(
                 out=z[:], in0=z[:], scalar=live[("rstd", it)][:, 0:1], in1=live[("gb", 1)][:], op0=ALU.mult, op1=ALU.add
             )
 
-        def op_C(a, eng):
-            it = a[0]
+        def z_leaky(it):
             z = live[("z", it)]
-            pieces = LAST_PIECES if it == LAST_TILE else 1
+            pieces = 2 if it == NT - 1 else 1
             width = D // pieces
             for c in range(pieces):
                 cs = slice(c * width, (c + 1) * width)
-                nc.vector.scalar_tensor_tensor(out=z[:, cs], in0=z[:, cs], scalar=SLOPE, in1=z[:, cs], op0=ALU.mult, op1=ALU.max)
+                V.scalar_tensor_tensor(out=z[:, cs], in0=z[:, cs], scalar=SLOPE, in1=z[:, cs], op0=ALU.mult, op1=ALU.max)
                 nc.sync.dma_start(out=out_v[:, it, cs], in_=z[:, cs])
 
-        table = {
-            "GBp": op_GBp, "RG": op_RG, "FQ": op_FQ, "Lp": op_Lp, "Ls": op_Ls, "Lv": op_Lv, "Wp": op_Wp, "Ws": op_Ws,
-            "Wv": op_Wv, "M1p": op_M1p, "M1s": op_M1s, "M1v": op_M1v, "M2p": op_M2p, "S1": op_S1, "NM": op_NM,
-            "S2": op_S2, "SQ": op_SQ, "A": op_A, "B": op_B, "C": op_C,
-        }
-        for kind, args, eng in ORDER:
-            table[kind](args, eng)
+        for g in range(2):
+            for g2 in range(2):
+                f_group(V, g, g2, 0, 2)
+                f_group(S, g, g2, 2, 4)
+                f_quant(g, g2)
+        gb_broadcast()
+        l_turn(0)
+        l_out(S, 0)
+        l_quant(0)
+        w_turn(0)
+        w_turn(1)
+        for pr in (0, 1):
+            w_out(S, pr, 0)
+            w_out(S, pr, 1)
+        w_quant(0)
+        m_mul(0)
+        m_out(S, 0, 0)
+        m_out(S, 0, 1)
+        m_quant(0)
+        l_turn(1)
+        l_out(S, 1)
+        l_quant(1)
+        w_turn(2)
+        w_turn(3)
+        for pr in (2, 3):
+            w_out(S, pr, 0)
+            w_out(V, pr, 1)
+        w_quant(1)
+        l_turn(2)
+        l_out(S, 2)
+        m_mul(1)
+        m_out(S, 1, 0)
+        m_out(V, 1, 1)
+        l_quant(2)
+        m_quant(1)
+        y_mul(0, 0)
+        y_mul(0, 1)
+        y_out(0, 0)
+        y_out(0, 1)
+        y_mean(0)
+        l_turn(3)
+        l_out(S, 3)
+        m_mul(2)
+        m_out(V, 2, 0)
+        m_out(V, 2, 1)
+        l_quant(3)
+        y_mul(1, 0)
+        y_mul(1, 1)
+        l_turn(4)
+        z_gamma(0)
+        m_quant(2)
+        for it in range(1, NT + 1):
+            if it + 2 < NT:
+                m_mul(it + 2)
+            if it + 1 < NT:
+                y_mul(it + 1, 0)
+                y_mul(it + 1, 1)
+            if it + 4 < NT:
+                l_turn(it + 4)
+            y_square(it - 1)
+            if it < NT:
+                y_out(it, 0)
+                y_out(it, 1)
+            y_rstd(it - 1)
+            if it + 3 < NT:
+                l_out(S, it + 3)
+            if it + 2 < NT:
+                m_out(S, it + 2, 0)
+                if it != 2:
+                    m_out(S, it + 2, 1)
+            if it < NT:
+                y_mean(it)
+            if it == 2:
+                m_out(V, it + 2, 1)
+            z_beta(it - 1)
+            if it + 3 < NT:
+                l_quant(it + 3)
+            if it < NT:
+                z_gamma(it)
+            if it + 2 < NT:
+                m_quant(it + 2)
+            z_leaky(it - 1)

@@ -40,7 +40,7 @@ def tile_gcn_pb_kernel(tc, lap, feat, w, gamma, beta, out):
         S.activation(out=warm[:], in_=eps_t[:], func=ACT.Abs_reciprocal_sqrt)
         ident = keep.tile([P, P], F32)
         make_identity(nc, ident[:])
-        ones = keep.tile([P, P], BF16)
+        ones = keep.tile([P, 512], BF16)
         V.memset(ones[:], 1.0)
 
         fr = keep.tile([P, 2, 2, 4, 512], BF16)
@@ -104,15 +104,19 @@ def tile_gcn_pb_kernel(tc, lap, feat, w, gamma, beta, out):
             else:
                 S.copy(out=dst, in_=src)
 
-        def gb_broadcast():
-            for k in range(2):
-                bank = psum.tile([P, D], BF16, name="gb%d" % k, tag="gb%d" % k, bufs=1)
-                for h in range(2):
-                    c0 = D * k + 512 * h
-                    nc.tensor.matmul(
-                        out=bank[:, 512 * h : 512 * h + 512], lhsT=ones[:], rhs=gb_row[:, c0 : c0 + 512], start=True, stop=True
-                    )
-                live[("gb", k)] = bank
+        for k in range(2):
+            live[("gb", k)] = psum.tile([P, D], BF16, name="gb%d" % k, tag="gb%d" % k, bufs=1)
+
+        def warm_up(n):
+            for i in range(n):
+                nc.tensor.matmul(out=live[("gb", 1)][:, 0:512], lhsT=ones[:, 0:P], rhs=ones[:], start=True, stop=True)
+
+        def gb_broadcast(k):
+            for h in range(2):
+                c0 = 512 * h
+                nc.tensor.matmul(
+                    out=live[("gb", k)][:, c0 : c0 + 512], lhsT=ones[:, 0:P], rhs=gb_row[:, D * k + c0 : D * k + c0 + 512], start=True, stop=True
+                )
 
         def f_group(eng, g, g2, s0, s1):
             src = fr[:, g, g2].rearrange("p t (c i s) -> p s c t i", i=2, s=4)
@@ -264,11 +268,12 @@ def tile_gcn_pb_kernel(tc, lap, feat, w, gamma, beta, out):
                 f_group(V, g, g2, 0, 2)
                 f_group(S, g, g2, 2, 4)
                 f_quant(g, g2)
-        gb_broadcast()
+        warm_up(16)
         l_turn(0)
         l_out(S, 0)
         l_quant(0)
         w_turn(0)
+        gb_broadcast(0)
         w_turn(1)
         for pr in (0, 1):
             w_out(S, pr, 0)
@@ -282,6 +287,7 @@ def tile_gcn_pb_kernel(tc, lap, feat, w, gamma, beta, out):
         l_out(S, 1)
         l_quant(1)
         w_turn(2)
+        gb_broadcast(1)
         w_turn(3)
         for pr in (2, 3):
             w_out(S, pr, 0)

@@ -256,7 +256,7 @@ def tile_gcn_pb_kernel(tc, lap, feat, w, gamma, beta, out):
 
         def z_leaky(it):
             z = live[("z", it)]
-            pieces = 2 if it == NT - 1 else 1
+            pieces = 4 if it == NT - 1 else 1
             width = D // pieces
             for c in range(pieces):
                 cs = slice(c * width, (c + 1) * width)
@@ -319,11 +319,11 @@ def tile_gcn_pb_kernel(tc, lap, feat, w, gamma, beta, out):
         for it in range(1, NT + 1):
             if it + 2 < NT:
                 m_mul(it + 2)
+            if it + 4 < NT:
+                l_turn(it + 4)
             if it + 1 < NT:
                 y_mul(it + 1, 0)
                 y_mul(it + 1, 1)
-            if it + 4 < NT:
-                l_turn(it + 4)
             y_square(it - 1)
             if it < NT:
                 y_out(it, 0)

@@ -268,26 +268,26 @@ def tile_gcn_pb_kernel(tc, lap, feat, w, gamma, beta, out):
                 f_group(V, g, g2, 0, 2)
                 f_group(S, g, g2, 2, 4)
                 f_quant(g, g2)
-        warm_up(16)
+        warm_up(12)
+        gb_broadcast(1)
         l_turn(0)
+        gb_broadcast(0)
         l_out(S, 0)
         l_quant(0)
         w_turn(0)
-        gb_broadcast(0)
         w_turn(1)
         for pr in (0, 1):
             w_out(S, pr, 0)
             w_out(S, pr, 1)
         w_quant(0)
+        l_turn(1)
         m_mul(0)
         m_out(S, 0, 0)
-        m_out(S, 0, 1)
+        m_out(V, 0, 1)
         m_quant(0)
-        l_turn(1)
         l_out(S, 1)
         l_quant(1)
         w_turn(2)
-        gb_broadcast(1)
         w_turn(3)
         for pr in (2, 3):
             w_out(S, pr, 0)
@@ -305,6 +305,7 @@ def tile_gcn_pb_kernel(tc, lap, feat, w, gamma, beta, out):
         y_out(0, 0)
         y_out(0, 1)
         y_mean(0)
+        z_gamma(0)
         l_turn(3)
         l_out(S, 3)
         m_mul(2)
@@ -314,7 +315,6 @@ def tile_gcn_pb_kernel(tc, lap, feat, w, gamma, beta, out):
         y_mul(1, 0)
         y_mul(1, 1)
         l_turn(4)
-        z_gamma(0)
         m_quant(2)
         for it in range(1, NT + 1):
             if it + 2 < NT:

@@ -250,9 +250,13 @@ def tile_gcn_pb_kernel(tc, lap, feat, w, gamma, beta, out):
 
         def z_beta(it):
             z = live[("z", it)]
-            V.scalar_tensor_tensor(
-                out=z[:], in0=z[:], scalar=live[("rstd", it)][:, 0:1], in1=live[("gb", 1)][:], op0=ALU.mult, op1=ALU.add
-            )
+            pieces = 2 if it == NT - 1 else 1
+            width = D // pieces
+            for c in range(pieces):
+                cs = slice(c * width, (c + 1) * width)
+                V.scalar_tensor_tensor(
+                    out=z[:, cs], in0=z[:, cs], scalar=live[("rstd", it)][:, 0:1], in1=live[("gb", 1)][:, cs], op0=ALU.mult, op1=ALU.add
+                )
 
         def z_leaky(it):
             z = live[("z", it)]
@@ -263,13 +267,14 @@ def tile_gcn_pb_kernel(tc, lap, feat, w, gamma, beta, out):
                 V.scalar_tensor_tensor(out=z[:, cs], in0=z[:, cs], scalar=SLOPE, in1=z[:, cs], op0=ALU.mult, op1=ALU.max)
                 nc.sync.dma_start(out=out_v[:, it, cs], in_=z[:, cs])
 
-        for g in range(2):
-            for g2 in range(2):
-                f_group(V, g, g2, 0, 2)
-                f_group(S, g, g2, 2, 4)
-                f_quant(g, g2)
-        warm_up(12)
-        gb_broadcast(1)
+        quarters = [(g, g2) for g in range(2) for g2 in range(2)]
+        for n, (g, g2) in enumerate(quarters):
+            f_group(V, g, g2, 0, 2)
+            f_group(S, g, g2, 2, 4)
+            if n >= 1:
+                f_quant(*quarters[n - 1])
+        f_quant(*quarters[-1])
+        warm_up(14)
         l_turn(0)
         gb_broadcast(0)
         l_out(S, 0)
@@ -278,7 +283,7 @@ def tile_gcn_pb_kernel(tc, lap, feat, w, gamma, beta, out):
         w_turn(1)
         for pr in (0, 1):
             w_out(S, pr, 0)
-            w_out(S, pr, 1)
+            w_out(V, pr, 1)
         w_quant(0)
         l_turn(1)
         m_mul(0)
@@ -288,6 +293,7 @@ def tile_gcn_pb_kernel(tc, lap, feat, w, gamma, beta, out):
         l_out(S, 1)
         l_quant(1)
         w_turn(2)
+        gb_broadcast(1)
         w_turn(3)
         for pr in (2, 3):
             w_out(S, pr, 0)
@@ -333,12 +339,9 @@ def tile_gcn_pb_kernel(tc, lap, feat, w, gamma, beta, out):
                 l_out(S, it + 3)
             if it + 2 < NT:
                 m_out(S, it + 2, 0)
-                if it != 2:
-                    m_out(S, it + 2, 1)
+                m_out(S, it + 2, 1)
             if it < NT:
                 y_mean(it)
-            if it == 2:
-                m_out(V, it + 2, 1)
             z_beta(it - 1)
             if it + 3 < NT:
                 l_quant(it + 3)

@@ -43,14 +43,19 @@ def tile_gcn_pb_kernel(tc, lap, feat, w, gamma, beta, out):
         ones = keep.tile([P, 512], BF16)
         V.memset(ones[:], 1.0)
 
-        fr = keep.tile([P, 2, 2, 4, 512], BF16)
+        fr0 = keep.tile([P, 2, 4, 512], BF16)
+        fr1 = keep.tile([P, 4, D], BF16)
         lap_sb = keep.tile([P, NT, N], BF16)
         w_sb = keep.tile([P, NT, D], BF16)
         lap_v = lap.rearrange("(p t) j -> p t j", t=NT)
 
-        def load_f(g, g2):
-            rows = feat[512 * g : 512 * g + 512, :].rearrange("(q t) c -> q t c", t=4)
-            nc.sync.dma_start(out=fr[:, g, g2], in_=rows[:, :, 512 * g2 : 512 * g2 + 512])
+        feat_v = feat.rearrange("(g q t) c -> g q t c", g=2, t=4)
+
+        def load_f0(g2):
+            nc.sync.dma_start(out=fr0[:, g2], in_=feat_v[0][:, :, 512 * g2 : 512 * g2 + 512])
+
+        def load_f1():
+            nc.sync.dma_start(out=fr1[:], in_=feat_v[1])
 
         def load_gb(k, vec):
             nc.sync.dma_start(out=gb_row[0:1, D * k : D * k + D], in_=vec.rearrange("(o d) -> o d", o=1))
@@ -58,18 +63,17 @@ def tile_gcn_pb_kernel(tc, lap, feat, w, gamma, beta, out):
         def load_w(k):
             nc.sync.dma_start(
                 out=w_sb[:, 2 * k : 2 * k + 2, :],
-                in_=w[256 * k : 256 * k + 256, :].rearrange("(t p) d -> p t d", p=P),
+                in_=w[256 * k : 256 * k + 256, :].rearrange("(p b) d -> p b d", b=2),
             )
 
         def load_l(t0, t1):
             nc.sync.dma_start(out=lap_sb[:, t0:t1, :], in_=lap_v[:, t0:t1, :])
 
-        load_f(0, 0)
-        load_f(0, 1)
+        load_f0(0)
+        load_f0(1)
         load_gb(0, gamma)
         load_gb(1, beta)
-        load_f(1, 0)
-        load_f(1, 1)
+        load_f1()
         load_l(0, 1)
         load_w(0)
         load_w(1)
@@ -119,7 +123,8 @@ def tile_gcn_pb_kernel(tc, lap, feat, w, gamma, beta, out):
                 )
 
         def f_group(eng, g, g2, s0, s1):
-            src = fr[:, g, g2].rearrange("p t (c i s) -> p s c t i", i=2, s=4)
+            rows = fr0[:, g2] if g == 0 else fr1[:, :, 512 * g2 : 512 * g2 + 512]
+            src = rows.rearrange("p t (c i s) -> p s c t i", i=2, s=4)
             dst = fg[:, g, 512 * g2 : 512 * g2 + 512, :].rearrange("p (s c i) t -> p s c t i", s=4, i=2)
             if eng is V:
                 V.tensor_copy(out=dst[:, s0:s1], in_=src[:, s0:s1])
@@ -160,7 +165,11 @@ def tile_gcn_pb_kernel(tc, lap, feat, w, gamma, beta, out):
                 live[("W", pr, g2)] = tp
 
         def w_out(eng, pr, g2):
-            copy_on(eng, wg_w[:, g2, 256 * pr : 256 * pr + 256, :], live[("W", pr, g2)][:].rearrange("p u b o -> p (b o) u"))
+            copy_on(
+                eng,
+                wg_w[:, g2, 256 * pr : 256 * pr + 256, :].rearrange("p (o b) u -> p o b u", b=2),
+                live[("W", pr, g2)][:].rearrange("p u b o -> p o b u"),
+            )
 
         def w_quant(h):
             cs = slice(512 * h, 512 * h + 512)

from contextlib import ExitStack

import concourse.mybir as mybir
from concourse.masks import make_identity

F32 = mybir.dt.float32
BF16 = mybir.dt.bfloat16
U32 = mybir.dt.uint32
U8 = mybir.dt.uint8
FP8X4 = mybir.dt.float8_e4m3fn_x4
ALU = mybir.AluOpType
ACT = mybir.ActivationFunctionType

P = 128
N = 1024
D = 1024
NT = N // P
EPS = 1e-5
SLOPE = 0.1
FLOPS = 2 * 2 * N * N * D


def tile_gcn_pb_kernel(tc, lap, feat, w, gamma, beta, out):
    nc = tc.nc
    V, S = nc.vector, nc.scalar
    with ExitStack() as ctx:
        keep = ctx.enter_context(tc.tile_pool(name="keep", bufs=1))
        ypool = ctx.enter_context(tc.tile_pool(name="ypool", bufs=4))
        opool = ctx.enter_context(tc.tile_pool(name="opool", bufs=4))
        small = ctx.enter_context(tc.tile_pool(name="small", bufs=6))
        psum = ctx.enter_context(tc.psum_pool(name="psum", bufs=6))
        ctx.enter_context(tc.manual_schedule())

        gb_row = keep.tile([P, 2 * D], BF16)
        V.memset(gb_row[:, 0:D], 0.0)
        nc.gpsimd.memset(gb_row[:, D : 2 * D], 0.0)
        eps_t = keep.tile([P, 1], F32)
        V.memset(eps_t[:], EPS)
        warm = keep.tile([P, 1], F32)
        S.activation(out=warm[:], in_=eps_t[:], func=ACT.Abs_reciprocal_sqrt)
        ident = keep.tile([P, P], F32)
        make_identity(nc, ident[:])
        ones = keep.tile([P, 512], BF16)
        V.memset(ones[:], 1.0)

        fr0 = keep.tile([P, 2, 4, 512], BF16)
        fr1 = keep.tile([P, 4, D], BF16)
        lap_sb = keep.tile([P, NT, N], BF16)
        w_sb = keep.tile([P, NT, D], BF16)
        lap_v = lap.rearrange("(p t) j -> p t j", t=NT)

        feat_v = feat.rearrange("(g q t) c -> g q t c", g=2, t=4)

        def load_f0(g2):
            nc.sync.dma_start(out=fr0[:, g2], in_=feat_v[0][:, :, 512 * g2 : 512 * g2 + 512])

        def load_f1():
            nc.sync.dma_start(out=fr1[:], in_=feat_v[1])

        def load_gb(k, vec):
            nc.sync.dma_start(out=gb_row[0:1, D * k : D * k + D], in_=vec.rearrange("(o d) -> o d", o=1))

        def load_w(k):
            nc.sync.dma_start(
                out=w_sb[:, 2 * k : 2 * k + 2, :],
                in_=w[256 * k : 256 * k + 256, :].rearrange("(p b) d -> p b d", b=2),
            )

        def load_l(t0, t1):
            nc.sync.dma_start(out=lap_sb[:, t0:t1, :], in_=lap_v[:, t0:t1, :])

        load_f0(0)
        load_f0(1)
        load_gb(0, gamma)
        load_gb(1, beta)
        load_f1()
        load_l(0, 1)
        load_w(0)
        load_w(1)
        load_l(1, 2)
        load_w(2)
        load_w(3)
        load_l(2, 4)
        load_l(4, 8)
        lap_w = lap_sb[:].bitcast(F32)
        w_w = w_sb[:].bitcast(F32)

        fg = keep.tile([P, 2, D, 4], BF16, align_bytes=64)
        f_codes = keep.tile([P, 2, D], U32, align_bytes=64)
        f_sc = keep.tile([P, 2, D], U8, align_bytes=64)
        lg = keep.tile([P, NT, 2, P, 4], BF16, align_bytes=64)
        lg_w = lg[:].bitcast(F32)
        l_codes = keep.tile([P, NT, 2, P], U32, align_bytes=64)
        l_sc = keep.tile([P, NT, 2, P], U8, align_bytes=64)
        wg = keep.tile([P, 2, D, 4], BF16, align_bytes=64)
        wg_w = wg[:].bitcast(F32)
        w_codes = keep.tile([P, 2, D], U32, align_bytes=64)
        w_sc = keep.tile([P, 2, D], U8, align_bytes=64)
        mg = keep.tile([P, NT, 2, P, 4], BF16, align_bytes=64)
        m_codes = keep.tile([P, NT, 2, P], U32, align_bytes=64)
        m_sc = keep.tile([P, NT, 2, P], U8, align_bytes=64)
        out_v = out.rearrange("(p t) o -> p t o", t=NT)
        live = {}

        def copy_on(eng, dst, src):
            if eng is V:
                V.tensor_copy(out=dst, in_=src)
            else:
                S.copy(out=dst, in_=src)

        for k in range(2):
            live[("gb", k)] = psum.tile([P, D], BF16, name="gb%d" % k, tag="gb%d" % k, bufs=1)

        def warm_up(n):
            for i in range(n):
                nc.tensor.matmul(out=live[("gb", 1)][:, 0:512], lhsT=ones[:, 0:P], rhs=ones[:], start=True, stop=True)

        def gb_broadcast(k):
            for h in range(2):
                c0 = 512 * h
                nc.tensor.matmul(
                    out=live[("gb", k)][:, c0 : c0 + 512], lhsT=ones[:, 0:P], rhs=gb_row[:, D * k + c0 : D * k + c0 + 512], start=True, stop=True
                )

        def f_group(eng, g, g2, s0, s1):
            rows = fr0[:, g2] if g == 0 else fr1[:, :, 512 * g2 : 512 * g2 + 512]
            src = rows.rearrange("p t (c i s) -> p s c t i", i=2, s=4)
            dst = fg[:, g, 512 * g2 : 512 * g2 + 512, :].rearrange("p (s c i) t -> p s c t i", s=4, i=2)
            if eng is V:
                V.tensor_copy(out=dst[:, s0:s1], in_=src[:, s0:s1])
            else:
                for s in range(s0, s1):
                    S.copy(out=dst[:, s], in_=src[:, s])

        def f_quant(g, g2):
            cs = slice(512 * g2, 512 * g2 + 512)
            V.quantize_mx(
                out=f_codes[:, g, cs].bitcast(FP8X4), scales=f_sc[:, g, cs], in_=fg[:, g, cs, :].rearrange("p c t -> p (c t)")
            )

        def l_turn(it):
            tp = psum.tile([P, 2, 2, P], F32, name="tp", tag="ps")
            for g in range(2):
                for u in range(2):
                    nc.tensor.transpose(tp[:, g, u, :], lap_w[:, it, 256 * g + u : 256 * g + 256 : 2], ident[:])
            live[("L", it)] = tp

        def l_out(eng, it):
            copy_on(eng, lg_w[:, it], live[("L", it)][:].rearrange("p g u i -> p g i u"))

        def l_quant(it):
            V.quantize_mx(
                out=l_codes[:, it].rearrange("p g i -> p (g i)").bitcast(FP8X4),
                scales=l_sc[:, it].rearrange("p g i -> p (g i)"),
                in_=lg[:, it].rearrange("p g i t -> p (g i t)"),
            )

        def w_turn(pr):
            for g2 in range(2):
                tp = psum.tile([P, 2, 2, P], F32, name="tp", tag="ps")
                for b in range(2):
                    for u in range(2):
                        words = w_w[:, 2 * pr + b, 256 * g2 + u : 256 * g2 + 256 : 2]
                        nc.tensor.transpose(tp[:, u, b, :], words, ident[:])
                live[("W", pr, g2)] = tp

        def w_out(eng, pr, g2):
            copy_on(
                eng,
                wg_w[:, g2, 256 * pr : 256 * pr + 256, :].rearrange("p (o b) u -> p o b u", b=2),
                live[("W", pr, g2)][:].rearrange("p u b o -> p o b u"),
            )

        def w_quant(h):
            cs = slice(512 * h, 512 * h + 512)
            for g2 in range(2):
                V.quantize_mx(
                    out=w_codes[:, g2, cs].bitcast(FP8X4), scales=w_sc[:, g2, cs], in_=wg[:, g2, cs, :].rearrange("p c t -> p (c t)")
                )

        def m_mul(it):
            for g2 in range(2):
                mp = psum.tile([P, 4, P], F32, name="mp", tag="ps")
                for t2 in range(4):
                    cs = slice((4 * g2 + t2) * P, (4 * g2 + t2 + 1) * P)
                    for g in range(2):
                        nc.tensor.matmul_mx(
                            out=mp[:, t2, :],
                            lhsT=f_codes[:, g, cs].bitcast(FP8X4),
                            lhsT_scale=f_sc[:, g, cs],
                            rhs=l_codes[:, it, g, :].bitcast(FP8X4),
                            rhs_scale=l_sc[:, it, g, :],
                            start=(g == 0),
                            stop=(g == 1),
                        )
                live[("M", it, g2)] = mp

        def m_out(eng, it, g2):
            copy_on(eng, mg[:, it, g2], live[("M", it, g2)][:].rearrange("p t i -> p i t"))

        def m_quant(it):
            V.quantize_mx(
                out=m_codes[:, it].rearrange("p g i -> p (g i)").bitcast(FP8X4),
                scales=m_sc[:, it].rearrange("p g i -> p (g i)"),
                in_=mg[:, it].rearrange("p g i t -> p (g i t)"),
            )

        def y_mul(it, h):
            yp = psum.tile([P, 512], F32, name="yp", tag="ps")
            cs = slice(512 * h, 512 * h + 512)
            for g2 in range(2):
                nc.tensor.matmul_mx(
                    out=yp[:],
                    lhsT=m_codes[:, it, g2, :].bitcast(FP8X4),
                    lhsT_scale=m_sc[:, it, g2, :],
                    rhs=w_codes[:, g2, cs].bitcast(FP8X4),
                    rhs_scale=w_sc[:, g2, cs],
                    start=(g2 == 0),
                    stop=(g2 == 1),
                )
            live[("Y", it, h)] = yp

        def y_out(it, h):
            if h == 0:
                live[("ysb", it)] = ypool.tile([P, D], F32, name="y_sb", tag="y_sb")
                live[("sums", it)] = small.tile([P, 2], F32, name="sums", tag="sums")
            S.activation(
                out=live[("ysb", it)][:, 512 * h : 512 * h + 512],
                in_=live[("Y", it, h)][:],
                func=ACT.Copy,
                accum_out=live[("sums", it)][:, h : h + 1],
            )

        def y_mean(it):
            negmu = small.tile([P, 1], F32, name="negmu", tag="negmu")
            sums = live[("sums", it)]
            V.tensor_scalar(out=negmu[:], in0=sums[:, 0:1], scalar1=sums[:, 1:2], scalar2=-1.0 / D, op0=ALU.add, op1=ALU.mult)
            live[("negmu", it)] = negmu

        def y_square(it):
            ssq = small.tile([P, 1], F32, name="ssq", tag="ssq")
            junk = keep.tile([P, D], BF16, name="junk", tag="junk")
            S.activation(
                out=junk[:], in_=live[("ysb", it)][:], func=ACT.Square, bias=live[("negmu", it)][:, 0:1], scale=1.0, accum_out=ssq[:]
            )
            live[("ssq", it)] = ssq

        def y_rstd(it):
            rstd = small.tile([P, 1], F32, name="rstd", tag="rstd")
            S.activation(out=rstd[:], in_=live[("ssq", it)][:], func=ACT.Abs_reciprocal_sqrt, bias=eps_t[:, 0:1], scale=1.0 / D)
            live[("rstd", it)] = rstd

        def z_gamma(it):
            z = opool.tile([P, D], F32, name="z", tag="z")
            V.scalar_tensor_tensor(
                out=z[:], in0=live[("ysb", it)][:], scalar=live[("negmu", it)][:, 0:1], in1=live[("gb", 0)][:], op0=ALU.add, op1=ALU.mult
            )
            live[("z", it)] = z

        def z_beta(it):
            z = live[("z", it)]
            pieces = 2 if it == NT - 1 else 1
            width = D // pieces
            for c in range(pieces):
                cs = slice(c * width, (c + 1) * width)
                V.scalar_tensor_tensor(
                    out=z[:, cs], in0=z[:, cs], scalar=live[("rstd", it)][:, 0:1], in1=live[("gb", 1)][:, cs], op0=ALU.mult, op1=ALU.add
                )

        def z_leaky(it):
            z = live[("z", it)]
            pieces = 4 if it == NT - 1 else 1
            width = D // pieces
            for c in range(pieces):
                cs = slice(c * width, (c + 1) * width)
                V.scalar_tensor_tensor(out=z[:, cs], in0=z[:, cs], scalar=SLOPE, in1=z[:, cs], op0=ALU.mult, op1=ALU.max)
                nc.sync.dma_start(out=out_v[:, it, cs], in_=z[:, cs])

        quarters = [(g, g2) for g in range(2) for g2 in range(2)]
        for n, (g, g2) in enumerate(quarters):
            f_group(V, g, g2, 0, 2)
            f_group(S, g, g2, 2, 4)
            if n >= 1:
                f_quant(*quarters[n - 1])
        f_quant(*quarters[-1])
        warm_up(14)
        l_turn(0)
        gb_broadcast(0)
        l_out(S, 0)
        l_quant(0)
        w_turn(0)
        w_turn(1)
        for pr in (0, 1):
            w_out(S, pr, 0)
            w_out(V, pr, 1)
        w_quant(0)
        l_turn(1)
        m_mul(0)
        m_out(S, 0, 0)
        m_out(V, 0, 1)
        m_quant(0)
        l_out(S, 1)
        l_quant(1)
        w_turn(2)
        gb_broadcast(1)
        w_turn(3)
        for pr in (2, 3):
            w_out(S, pr, 0)
            w_out(V, pr, 1)
        w_quant(1)
        l_turn(2)
        l_out(S, 2)
        m_mul(1)
        m_out(S, 1, 0)
        m_out(V, 1, 1)
        l_quant(2)
        m_quant(1)
        y_mul(0, 0)
        y_mul(0, 1)
        y_out(0, 0)
        y_out(0, 1)
        y_mean(0)
        z_gamma(0)
        l_turn(3)
        l_out(S, 3)
        m_mul(2)
        m_out(V, 2, 0)
        m_out(V, 2, 1)
        l_quant(3)
        y_mul(1, 0)
        y_mul(1, 1)
        l_turn(4)
        m_quant(2)
        for it in range(1, NT + 1):
            if it + 2 < NT:
                m_mul(it + 2)
            if it + 4 < NT:
                l_turn(it + 4)
            if it + 1 < NT:
                y_mul(it + 1, 0)
                y_mul(it + 1, 1)
            y_square(it - 1)
            if it < NT:
                y_out(it, 0)
                y_out(it, 1)
            y_rstd(it - 1)
            if it + 3 < NT:
                l_out(S, it + 3)
            if it + 2 < NT:
                m_out(S, it + 2, 0)
                m_out(S, it + 2, 1)
            if it < NT:
                y_mean(it)
            z_beta(it - 1)
            if it + 3 < NT:
                l_quant(it + 3)
            if it < NT:
                z_gamma(it)
            if it + 2 < NT:
                m_quant(it + 2)
            z_leaky(it - 1)
